import numpy as np
import ml_dtypes

BF16 = ml_dtypes.bfloat16


def bf(x):
    return np.asarray(x, np.float32).astype(BF16)


def f32(x):
    return np.asarray(x, np.float32)


def f64(x):
    return np.asarray(x).astype(np.float64)


def striped(idx):
    return np.tile(idx.reshape(-1, 16).T, (8, 1))


C, S, N, L = 128, 4096, 2304, 4
R = np.sqrt(0.5)
LEN = [S >> (k + 1) for k in range(L)] + [S >> L]
REV = LEN[::-1]


def wavedec(y):
    details = []
    cur = y
    for _ in range(L):
        p = cur.reshape(cur.shape[0], -1, 2)
        details.append((p[..., 0] - p[..., 1]) * R)
        cur = (p[..., 0] + p[..., 1]) * R
    return np.concatenate([cur] + details[::-1], axis=-1)


def waverec(parts):
    a = parts[0]
    for d in parts[1:]:
        a = np.stack([(a + d) * R, (a - d) * R], axis=-1).reshape(a.shape[0], -1)
    return a


def setup_inputs():
    return {"x": f32(np.random.standard_normal((C, S))), "pre": f32(np.random.standard_normal((1, S))), "mid": f32(np.random.standard_normal((1, N))), "post": f32(np.random.standard_normal((1, S))), "offs": striped(np.random.permutation(S)[:N])}


def reference(x, pre, mid, post, offs):
    idx = offs[:16].T.reshape(-1)
    w = wavedec(f64(x) * f64(pre))
    t = w[:, idx] * f64(mid)
    parts = []
    start = 0
    for k in range(L + 1):
        parts.append(t[:, start:start + REV[k]])
        start = LEN[k]
    return waverec(parts) * f64(post)

@@ -1,0 +1,299 @@
+import math
+
+import concourse.mybir as mybir
+from concourse.masks import make_identity
+
+F32 = mybir.dt.float32
+U16 = mybir.dt.uint16
+ADD = mybir.AluOpType.add
+SUB = mybir.AluOpType.subtract
+MULT = mybir.AluOpType.mult
+COPY = mybir.ActivationFunctionType.Copy
+
+P = 128
+S = 4096
+N = 2304
+R = math.sqrt(0.5)
+ROOT = S // 16
+T_START = {0: 0, 1: 2048, 2: 1024, 3: 512, 4: 256}
+SIGNS = ((0, 1.0), (1, -1.0))
+
+GROUP = 4
+WIDE = GROUP * P
+GROUPS = S // WIDE
+IN_TENSOR = GROUPS // 2
+OUT_TENSOR = GROUPS // 2
+PIECE = 128
+
+FLOPS = P * (2 * S + N + 4 * (S - ROOT))
+
+
+def grouped(ap, g):
+    return ap.rearrange("p (j r) -> p j r", r=g)
+
+
+def across(ap, runs):
+    return ap.rearrange("p (r j) -> p j r", r=runs)
+
+
+def coefficient_places(n):
+    return [(0, n >> 4)] + [(n >> k, n >> k) for k in (4, 3, 2, 1)]
+
+
+def tile_waveletlayer_kernel(tc, x, pre, mid, post, offs, out):
+    nc = tc.nc
+    pre_row = pre.rearrange("o n -> (o n)")
+    mid_row = mid.rearrange("o n -> (o n)")
+    post_row = post.rearrange("o n -> (o n)")
+    in_vector = GROUPS - IN_TENSOR
+    split = IN_TENSOR * WIDE
+
+    with (
+        tc.tile_pool(name="held", bufs=1) as held,
+        tc.tile_pool(name="ring", bufs=3) as ring,
+        tc.psum_pool(name="psum", bufs=2) as psum,
+        tc.psum_pool(name="spreads", bufs=GROUPS - OUT_TENSOR) as spreads,
+    ):
+        offsets = held.tile([P, N // 16], U16, name="offsets")
+        nc.sync.dma_start(offsets[:], offs)
+        pre_rows = held.tile([S // P, P], F32, name="pre_rows")
+        nc.sync.dma_start(pre_rows[:], pre_row.rearrange("(b s) -> b s", s=P))
+        post_rows = held.tile([S // P, P], F32, name="post_rows")
+        nc.sync.dma_start(post_rows[:], post_row.rearrange("(b s) -> b s", s=P))
+        x_sb = held.tile([P, S], F32, name="x_sb")
+        for i in range(max(IN_TENSOR, in_vector)):
+            if i < IN_TENSOR:
+                nc.sync.dma_start(x_sb[:, i * WIDE : (i + 1) * WIDE], x[:, i * WIDE : (i + 1) * WIDE])
+            if i < in_vector:
+                nc.sync.dma_start(x_sb[:, split + i * WIDE : split + (i + 1) * WIDE], x[:, split + i * WIDE : split + (i + 1) * WIDE])
+        mid_sb = held.tile([P, N], F32, name="mid_sb")
+        mid_cut = T_START[4] + OUT_TENSOR * WIDE // 2
+        for cols in (slice(0, mid_cut), slice(mid_cut, N)):
+            nc.sync.dma_start(mid_sb[:, cols], mid_row[cols].partition_broadcast(P))
+
+        identity = held.tile([P, P], F32, name="identity")
+        make_identity(nc, identity[:])
+
+        def blocks_to_columns(rows, name):
+            blocks = rows.shape[0]
+            columns_ps = psum.tile([P, WIDE], F32, name="flipped_ps")
+            nc.tensor.matmul(columns_ps[:, 0:blocks], rows, identity[0:blocks, 0:blocks])
+            columns = held.tile([P, blocks], F32, name=name)
+            nc.scalar.activation(columns[:], columns_ps[:, 0:blocks], COPY)
+            return columns
+
+        def spread(columns, first):
+            spread_ps = spreads.tile([P, WIDE], F32, name="spread_ps")
+            for i in range(GROUP):
+                one = columns[:, first + i : first + i + 1]
+                nc.tensor.transpose(spread_ps[:, i * P : (i + 1) * P], one.to_broadcast([P, P]), identity[:])
+            return spread_ps
+
+        pre_cols = blocks_to_columns(pre_rows[:], "pre_cols")
+
+        post_cols = blocks_to_columns(post_rows[:], "post_cols")
+
+        haar = held.tile([P, P], F32, name="haar")
+        sums = identity
+        for k in (1, 2, 3, 4):
+            half = P >> k
+            two = grouped(sums[:], 2)
+            sums = held.tile([P, half], F32, name=f"impulse_sum{k}")
+            nc.gpsimd.tensor_tensor(sums[:], two[:, :, 0], two[:, :, 1], ADD)
+            diff = held.tile([P, half], F32, name=f"impulse_diff{k}")
+            nc.gpsimd.tensor_tensor(diff[:], two[:, :, 0], two[:, :, 1], SUB)
+            nc.scalar.mul(haar[:, half : 2 * half], diff[:], R**k)
+        nc.scalar.mul(haar[:, 0 : P >> 4], sums[:], R**4)
+
+        out_blocks = OUT_TENSOR * GROUP
+        haar_post = held.tile([P, out_blocks * P], F32, name="haar_post")
+        for b in range(out_blocks):
+            nc.vector.tensor_scalar_mul(haar_post[:, b * P : (b + 1) * P], haar[:], post_cols[:, b : b + 1])
+
+        w = held.tile([P, S], F32, name="w")
+        flipped = {}
+
+        def flip_x(g):
+            flipped_ps = psum.tile([P, WIDE], F32, name="flipped_ps")
+            flipped[g] = ring.tile([P, WIDE], F32, name="flipped")
+            for i in range(GROUP):
+                b = g * GROUP + i
+                nc.tensor.transpose(flipped_ps[:, i * P : (i + 1) * P], x_sb[:, b * P : (b + 1) * P], identity[:])
+            for i in range(GROUP):
+                b = g * GROUP + i
+                nc.scalar.mul(flipped[g][:, i * P : (i + 1) * P], flipped_ps[:, i * P : (i + 1) * P], pre_cols[:, b : b + 1])
+
+        def analyse_on_tensor(g):
+            product_ps = psum.tile([P, WIDE], F32, name="product_ps")
+            for i in range(GROUP):
+                nc.tensor.matmul(product_ps[:, i * P : (i + 1) * P], flipped[g][:, i * P : (i + 1) * P], haar[:])
+            for (in_block, count), in_w in zip(coefficient_places(P), coefficient_places(S)):
+                first = in_w[0] + g * GROUP * count
+                nc.scalar.activation(
+                    grouped(w[:, first : first + GROUP * count], count),
+                    grouped(product_ps[:], P)[:, :, in_block : in_block + count],
+                    COPY,
+                )
+
+        sums = {k: held.tile([P, (S - split) >> k], F32, name=f"sum{k}") for k in (0, 1, 2, 3)}
+        diffs = {k: held.tile([P, (S - split) >> k], F32, name=f"diff{k}") for k in (1, 2, 3)}
+
+        def scale(v):
+            pre_ps = spread(pre_cols, (IN_TENSOR + v) * GROUP)
+            nc.vector.scalar_tensor_tensor(
+                across(sums[0][:, v * WIDE : (v + 1) * WIDE], 2),
+                grouped(x_sb[:, split + v * WIDE : split + (v + 1) * WIDE], 2),
+                R**4,
+                grouped(pre_ps[:], 2),
+                MULT,
+                MULT,
+            )
+
+        def halve(k, two_runs, sum_to, first):
+            n = two_runs.shape[1] // 2
+            even, odd = two_runs[:, 0:n], two_runs[:, n : 2 * n]
+            d_k = slice((S >> k) + first, (S >> k) + first + n)
+            if k < 4:
+                nc.vector.tensor_tensor(sum_to, grouped(even, 2), grouped(odd, 2), ADD)
+                here = slice(first - (split >> k), first - (split >> k) + n)
+                nc.vector.tensor_tensor(diffs[k][:, here], even, odd, SUB)
+                nc.scalar.mul(w[:, d_k], diffs[k][:, here], R ** (k - 4))
+            else:
+                nc.vector.tensor_tensor(w[:, first : first + n], even, odd, ADD)
+                nc.vector.tensor_tensor(w[:, d_k], even, odd, SUB)
+
+        def first_level(v):
+            halve(1, sums[0][:, v * WIDE : (v + 1) * WIDE], across(sums[1][:, v * WIDE // 2 : (v + 1) * WIDE // 2], 2), (split + v * WIDE) >> 1)
+
+        def second_level(v):
+            rows = slice(v * WIDE // 8, (v + 1) * WIDE // 8)
+            halve(2, sums[1][:, v * WIDE // 2 : (v + 1) * WIDE // 2], across(sums[2][:], 2)[:, rows, :], (split + v * WIDE) >> 2)
+
+        for i in range(max(IN_TENSOR, in_vector) + 1):
+            if i < in_vector:
+                scale(i)
+            if i < IN_TENSOR:
+                flip_x(i)
+            if 0 < i <= IN_TENSOR:
+                analyse_on_tensor(i - 1)
+            if 0 < i <= in_vector:
+                second_level(i - 1)
+            if i < in_vector:
+                first_level(i)
+        halve(3, sums[2][:], across(sums[3][:], 2), split >> 3)
+        halve(4, sums[3][:], None, split >> 4)
+
+        synth = held.tile([P, out_blocks * P], F32, name="synth")
+        for g in range(OUT_TENSOR):
+            synth_ps = psum.tile([P, WIDE], F32, name="product_ps")
+            for i in range(GROUP):
+                b = g * GROUP + i
+                nc.tensor.transpose(synth_ps[:, i * P : (i + 1) * P], haar_post[:, b * P : (b + 1) * P], identity[:])
+            nc.scalar.activation(synth[:, g * WIDE : (g + 1) * WIDE], synth_ps[:], COPY)
+
+        post_ps = {g: spread(post_cols, g * GROUP) for g in range(OUT_TENSOR, GROUPS)}
+
+        t = held.tile([P, N], F32, name="t")
+        looked_up = []
+
+        def look_up(ranges):
+            lacking = sorted(
+                {p for first, last in ranges for p in range(first // PIECE, (last + PIECE - 1) // PIECE)} - set(looked_up)
+            )
+            looked_up.extend(lacking)
+            runs = []
+            for p in lacking:
+                if runs and runs[-1][1] == p:
+                    runs[-1][1] = p + 1
+                else:
+                    runs.append([p, p + 1])
+            for run in runs:
+                first, last = run[0] * PIECE, run[1] * PIECE
+                nc.vector.tensor_tensor(
+                    t[:, first:last], w[:].indirect(offsets[:, first // 16 : last // 16]), mid_sb[:, first:last], MULT
+                )
+
+        for g in range(OUT_TENSOR):
+            look_up(
+                [
+                    (T_START[k] + g * GROUP * place[1], T_START[k] + (g + 1) * GROUP * place[1])
+                    for k, place in enumerate(coefficient_places(P))
+                ]
+            )
+        look_up([(0, N)])
+
+        o_sb = held.tile([P, S], F32, name="o_sb")
+
+        def flip_t(g):
+            packed = ring.tile([P, WIDE], F32, name="packed")
+            for k, (in_block, count) in enumerate(coefficient_places(P)):
+                first = T_START[k] + g * GROUP * count
+                nc.scalar.activation(
+                    grouped(packed[:], P)[:, :, in_block : in_block + count],
+                    grouped(t[:, first : first + GROUP * count], count),
+                    COPY,
+                )
+            flipped_ps = psum.tile([P, WIDE], F32, name="flipped_ps")
+            for i in range(GROUP):
+                nc.tensor.transpose(flipped_ps[:, i * P : (i + 1) * P], packed[:, i * P : (i + 1) * P], identity[:])
+            flipped[g] = ring.tile([P, WIDE], F32, name="flipped")
+            nc.scalar.activation(flipped[g][:], flipped_ps[:], COPY)
+
+        def synthesise_on_tensor(g):
+            product_ps = psum.tile([P, WIDE], F32, name="product_ps")
+            for i in range(GROUP):
+                b = g * GROUP + i
+                nc.tensor.matmul(product_ps[:, i * P : (i + 1) * P], flipped[g][:, i * P : (i + 1) * P], synth[:, b * P : (b + 1) * P])
+            cols = slice(g * WIDE, (g + 1) * WIDE)
+            nc.scalar.activation(o_sb[:, cols], product_ps[:], COPY)
+            nc.scalar.dma_start(out[:, cols], o_sb[:, cols])
+
+        flip_t(0)
+        for g in range(OUT_TENSOR):
+            if g + 1 < OUT_TENSOR:
+                flip_t(g + 1)
+            synthesise_on_tensor(g)
+
+        halves = {k: held.tile([P, ROOT << k], F32, name=f"halves{k}") for k in (1, 2, 3, 4)}
+
+        def double(k, m0, m1):
+            g = 1 << (k - 1)
+            n = ROOT * g
+            f_k = t[:, T_START[k] + g * m0 : T_START[k] + g * m1]
+            for s, sign in SIGNS:
+                run = halves[k][:, s * n + g * m0 : s * n + g * m1]
+                if k == 1:
+                    nc.vector.scalar_tensor_tensor(run, f_k, sign, t[:, m0:m1], MULT, ADD)
+                else:
+                    nc.vector.scalar_tensor_tensor(
+                        grouped(run, 2),
+                        grouped(f_k, 2),
+                        sign * R ** (1 - k),
+                        across(halves[k - 1], 2)[:, g * m0 // 2 : g * m1 // 2, :],
+                        MULT,
+                        ADD,
+                    )
+
+        def finish(g):
+            cols = slice(g * WIDE, (g + 1) * WIDE)
+            nc.vector.scalar_tensor_tensor(
+                grouped(o_sb[:, cols], 2),
+                across(halves[4], 2)[:, g * WIDE // 2 : (g + 1) * WIDE // 2, :],
+                R**4,
+                grouped(post_ps[g][:], 2),
+                MULT,
+                MULT,
+            )
+            nc.sync.dma_start(out[:, cols], o_sb[:, cols])
+
+        roots = WIDE // 16
+        double(1, OUT_TENSOR * roots, ROOT)
+        double(2, OUT_TENSOR * roots, ROOT)
+        for step in range(OUT_TENSOR, GROUPS + 2):
+            for behind in range(3):
+                g = step - behind
+                if OUT_TENSOR <= g < GROUPS:
+                    if behind < 2:
+                        double(3 + behind, g * roots, (g + 1) * roots)
+                    else:
+                        finish(g)

@@ -22,8 +22,8 @@ GROUP = 4
 WIDE = GROUP * P
 GROUPS = S // WIDE
 IN_TENSOR = GROUPS // 2
-OUT_TENSOR = GROUPS // 2
-PIECE = 128
+OUT_TENSOR = 6
+OUT_TENSOR_ORDER = (2, 3, 1, 0, 4, 5)
 
 FLOPS = P * (2 * S + N + 4 * (S - ROOT))
 
@@ -52,14 +52,13 @@ def tile_waveletlayer_kernel(tc, x, pre, mid, post, offs, out):
         tc.tile_pool(name="held", bufs=1) as held,
         tc.tile_pool(name="ring", bufs=3) as ring,
         tc.psum_pool(name="psum", bufs=2) as psum,
-        tc.psum_pool(name="spreads", bufs=GROUPS - OUT_TENSOR) as spreads,
+        tc.psum_pool(name="products", bufs=3) as products,
+        tc.psum_pool(name="spreads", bufs=3) as spreads,
     ):
         offsets = held.tile([P, N // 16], U16, name="offsets")
         nc.sync.dma_start(offsets[:], offs)
         pre_rows = held.tile([S // P, P], F32, name="pre_rows")
         nc.sync.dma_start(pre_rows[:], pre_row.rearrange("(b s) -> b s", s=P))
-        post_rows = held.tile([S // P, P], F32, name="post_rows")
-        nc.sync.dma_start(post_rows[:], post_row.rearrange("(b s) -> b s", s=P))
         x_sb = held.tile([P, S], F32, name="x_sb")
         for i in range(max(IN_TENSOR, in_vector)):
             if i < IN_TENSOR:
@@ -67,9 +66,11 @@ def tile_waveletlayer_kernel(tc, x, pre, mid, post, offs, out):
             if i < in_vector:
                 nc.sync.dma_start(x_sb[:, split + i * WIDE : split + (i + 1) * WIDE], x[:, split + i * WIDE : split + (i + 1) * WIDE])
         mid_sb = held.tile([P, N], F32, name="mid_sb")
-        mid_cut = T_START[4] + OUT_TENSOR * WIDE // 2
-        for cols in (slice(0, mid_cut), slice(mid_cut, N)):
-            nc.sync.dma_start(mid_sb[:, cols], mid_row[cols].partition_broadcast(P))
+        nc.sync.dma_start(mid_sb[:], mid_row.partition_broadcast(P))
+        post_sb = held.tile([P, S], F32, name="post_sb")
+        for g in range(0, GROUPS, 2):
+            cols = slice(g * WIDE, (g + 2) * WIDE)
+            nc.sync.dma_start(post_sb[:, cols], post_row[cols].partition_broadcast(P))
 
         identity = held.tile([P, P], F32, name="identity")
         make_identity(nc, identity[:])
@@ -91,8 +92,6 @@ def tile_waveletlayer_kernel(tc, x, pre, mid, post, offs, out):
 
         pre_cols = blocks_to_columns(pre_rows[:], "pre_cols")
 
-        post_cols = blocks_to_columns(post_rows[:], "post_cols")
-
         haar = held.tile([P, P], F32, name="haar")
         sums = identity
         for k in (1, 2, 3, 4):
@@ -104,11 +103,6 @@ def tile_waveletlayer_kernel(tc, x, pre, mid, post, offs, out):
             nc.gpsimd.tensor_tensor(diff[:], two[:, :, 0], two[:, :, 1], SUB)
             nc.scalar.mul(haar[:, half : 2 * half], diff[:], R**k)
         nc.scalar.mul(haar[:, 0 : P >> 4], sums[:], R**4)
-
-        out_blocks = OUT_TENSOR * GROUP
-        haar_post = held.tile([P, out_blocks * P], F32, name="haar_post")
-        for b in range(out_blocks):
-            nc.vector.tensor_scalar_mul(haar_post[:, b * P : (b + 1) * P], haar[:], post_cols[:, b : b + 1])
 
         w = held.tile([P, S], F32, name="w")
         flipped = {}
@@ -124,7 +118,7 @@ def tile_waveletlayer_kernel(tc, x, pre, mid, post, offs, out):
                 nc.scalar.mul(flipped[g][:, i * P : (i + 1) * P], flipped_ps[:, i * P : (i + 1) * P], pre_cols[:, b : b + 1])
 
         def analyse_on_tensor(g):
-            product_ps = psum.tile([P, WIDE], F32, name="product_ps")
+            product_ps = products.tile([P, WIDE], F32, name="product_ps")
             for i in range(GROUP):
                 nc.tensor.matmul(product_ps[:, i * P : (i + 1) * P], flipped[g][:, i * P : (i + 1) * P], haar[:])
             for (in_block, count), in_w in zip(coefficient_places(P), coefficient_places(S)):
@@ -170,10 +164,10 @@ def tile_waveletlayer_kernel(tc, x, pre, mid, post, offs, out):
             halve(2, sums[1][:, v * WIDE // 2 : (v + 1) * WIDE // 2], across(sums[2][:], 2)[:, rows, :], (split + v * WIDE) >> 2)
 
         for i in range(max(IN_TENSOR, in_vector) + 1):
-            if i < in_vector:
-                scale(i)
             if i < IN_TENSOR:
                 flip_x(i)
+            if i < in_vector:
+                scale(i)
             if 0 < i <= IN_TENSOR:
                 analyse_on_tensor(i - 1)
             if 0 < i <= in_vector:
@@ -183,44 +177,28 @@ def tile_waveletlayer_kernel(tc, x, pre, mid, post, offs, out):
         halve(3, sums[2][:], across(sums[3][:], 2), split >> 3)
         halve(4, sums[3][:], None, split >> 4)
 
-        synth = held.tile([P, out_blocks * P], F32, name="synth")
-        for g in range(OUT_TENSOR):
-            synth_ps = psum.tile([P, WIDE], F32, name="product_ps")
-            for i in range(GROUP):
-                b = g * GROUP + i
-                nc.tensor.transpose(synth_ps[:, i * P : (i + 1) * P], haar_post[:, b * P : (b + 1) * P], identity[:])
-            nc.scalar.activation(synth[:, g * WIDE : (g + 1) * WIDE], synth_ps[:], COPY)
-
-        post_ps = {g: spread(post_cols, g * GROUP) for g in range(OUT_TENSOR, GROUPS)}
+        haar_t_ps = products.tile([P, WIDE], F32, name="product_ps")
+        nc.tensor.transpose(haar_t_ps[:, 0:P], haar[:], identity[:])
+        haar_t = held.tile([P, P], F32, name="haar_t")
+        nc.scalar.activation(haar_t[:], haar_t_ps[:, 0:P], COPY)
 
         t = held.tile([P, N], F32, name="t")
-        looked_up = []
 
-        def look_up(ranges):
-            lacking = sorted(
-                {p for first, last in ranges for p in range(first // PIECE, (last + PIECE - 1) // PIECE)} - set(looked_up)
+        def look_up(first, last):
+            nc.vector.tensor_tensor(
+                t[:, first:last], w[:].indirect(offsets[:, first // 16 : last // 16]), mid_sb[:, first:last], MULT
             )
-            looked_up.extend(lacking)
-            runs = []
-            for p in lacking:
-                if runs and runs[-1][1] == p:
-                    runs[-1][1] = p + 1
-                else:
-                    runs.append([p, p + 1])
-            for run in runs:
-                first, last = run[0] * PIECE, run[1] * PIECE
-                nc.vector.tensor_tensor(
-                    t[:, first:last], w[:].indirect(offsets[:, first // 16 : last // 16]), mid_sb[:, first:last], MULT
-                )
 
-        for g in range(OUT_TENSOR):
-            look_up(
-                [
-                    (T_START[k] + g * GROUP * place[1], T_START[k] + (g + 1) * GROUP * place[1])
-                    for k, place in enumerate(coefficient_places(P))
-                ]
-            )
-        look_up([(0, N)])
+        half = ROOT // 2
+        look_up(768, 1024)
+        look_up(0, half)
+        look_up(2048, 2048 + half)
+        look_up(1152, 1280)
+        look_up(1024, 1152)
+        look_up(256, 768)
+        look_up(half, ROOT)
+        look_up(2048 + half, N)
+        look_up(1280, 2048)
 
         o_sb = held.tile([P, S], F32, name="o_sb")
 
@@ -240,18 +218,17 @@ def tile_waveletlayer_kernel(tc, x, pre, mid, post, offs, out):
             nc.scalar.activation(flipped[g][:], flipped_ps[:], COPY)
 
         def synthesise_on_tensor(g):
-            product_ps = psum.tile([P, WIDE], F32, name="product_ps")
+            product_ps = products.tile([P, WIDE], F32, name="product_ps")
             for i in range(GROUP):
-                b = g * GROUP + i
-                nc.tensor.matmul(product_ps[:, i * P : (i + 1) * P], flipped[g][:, i * P : (i + 1) * P], synth[:, b * P : (b + 1) * P])
+                nc.tensor.matmul(product_ps[:, i * P : (i + 1) * P], flipped[g][:, i * P : (i + 1) * P], haar_t[:])
             cols = slice(g * WIDE, (g + 1) * WIDE)
-            nc.scalar.activation(o_sb[:, cols], product_ps[:], COPY)
-            nc.scalar.dma_start(out[:, cols], o_sb[:, cols])
+            nc.vector.tensor_tensor(o_sb[:, cols], product_ps[:], post_sb[:, cols], MULT)
+            nc.sync.dma_start(out[:, cols], o_sb[:, cols])
 
-        flip_t(0)
-        for g in range(OUT_TENSOR):
-            if g + 1 < OUT_TENSOR:
-                flip_t(g + 1)
+        flip_t(OUT_TENSOR_ORDER[0])
+        for g, next_g in zip(OUT_TENSOR_ORDER, OUT_TENSOR_ORDER[1:] + (None,)):
+            if next_g is not None:
+                flip_t(next_g)
             synthesise_on_tensor(g)
 
         halves = {k: held.tile([P, ROOT << k], F32, name=f"halves{k}") for k in (1, 2, 3, 4)}
@@ -280,7 +257,7 @@ def tile_waveletlayer_kernel(tc, x, pre, mid, post, offs, out):
                 grouped(o_sb[:, cols], 2),
                 across(halves[4], 2)[:, g * WIDE // 2 : (g + 1) * WIDE // 2, :],
                 R**4,
-                grouped(post_ps[g][:], 2),
+                grouped(post_sb[:, cols], 2),
                 MULT,
                 MULT,
             )

@@ -21,9 +21,10 @@ SIGNS = ((0, 1.0), (1, -1.0))
 GROUP = 4
 WIDE = GROUP * P
 GROUPS = S // WIDE
-IN_TENSOR = GROUPS // 2
-OUT_TENSOR = 6
-OUT_TENSOR_ORDER = (2, 3, 1, 0, 4, 5)
+SPLIT = 18 * P
+OUT_TENSOR = 5
+OUT_TENSOR_ORDER = (2, 3, 1, 0, 4)
+FOLDED = OUT_TENSOR_ORDER[:2]
 
 FLOPS = P * (2 * S + N + 4 * (S - ROOT))
 
@@ -45,26 +46,42 @@ def tile_waveletlayer_kernel(tc, x, pre, mid, post, offs, out):
     pre_row = pre.rearrange("o n -> (o n)")
     mid_row = mid.rearrange("o n -> (o n)")
     post_row = post.rearrange("o n -> (o n)")
-    in_vector = GROUPS - IN_TENSOR
-    split = IN_TENSOR * WIDE
+    tensor_portions = [(c, min(WIDE, SPLIT - c)) for c in range(0, SPLIT, WIDE)]
+    rest = (S - SPLIT - WIDE) // 2
+    vector_portions = [(SPLIT, WIDE), (SPLIT + WIDE, rest), (SPLIT + WIDE + rest, rest)]
 
     with (
         tc.tile_pool(name="held", bufs=1) as held,
         tc.tile_pool(name="ring", bufs=3) as ring,
+        tc.tile_pool(name="scaled", bufs=1) as scaled,
         tc.psum_pool(name="psum", bufs=2) as psum,
         tc.psum_pool(name="products", bufs=3) as products,
-        tc.psum_pool(name="spreads", bufs=3) as spreads,
     ):
         offsets = held.tile([P, N // 16], U16, name="offsets")
         nc.sync.dma_start(offsets[:], offs)
-        pre_rows = held.tile([S // P, P], F32, name="pre_rows")
-        nc.sync.dma_start(pre_rows[:], pre_row.rearrange("(b s) -> b s", s=P))
+        blocks = S // P
+        rows = held.tile([2 * blocks, P], F32, name="rows")
+        nc.sync.dma_start(rows[0:blocks, :], pre_row.rearrange("(b s) -> b s", s=P))
+        nc.sync.dma_start(rows[blocks : 2 * blocks, :], post_row.rearrange("(b s) -> b s", s=P))
         x_sb = held.tile([P, S], F32, name="x_sb")
-        for i in range(max(IN_TENSOR, in_vector)):
-            if i < IN_TENSOR:
-                nc.sync.dma_start(x_sb[:, i * WIDE : (i + 1) * WIDE], x[:, i * WIDE : (i + 1) * WIDE])
-            if i < in_vector:
-                nc.sync.dma_start(x_sb[:, split + i * WIDE : split + (i + 1) * WIDE], x[:, split + i * WIDE : split + (i + 1) * WIDE])
+        pre_sb = held.tile([P, S - SPLIT], F32, name="pre_sb")
+
+        def load_x(first, width):
+            nc.sync.dma_start(x_sb[:, first : first + width], x[:, first : first + width])
+
+        def load_pre_and_x(first, width):
+            here = first - SPLIT
+            nc.sync.dma_start(pre_sb[:, here : here + width], pre_row[first : first + width].partition_broadcast(P))
+            load_x(first, width)
+
+        load_x(*tensor_portions[0])
+        load_pre_and_x(*vector_portions[0])
+        load_x(*tensor_portions[1])
+        load_pre_and_x(*vector_portions[1])
+        load_x(*tensor_portions[2])
+        load_x(*tensor_portions[3])
+        load_pre_and_x(*vector_portions[2])
+        load_x(*tensor_portions[4])
         mid_sb = held.tile([P, N], F32, name="mid_sb")
         nc.sync.dma_start(mid_sb[:], mid_row.partition_broadcast(P))
         post_sb = held.tile([P, S], F32, name="post_sb")
@@ -75,22 +92,11 @@ def tile_waveletlayer_kernel(tc, x, pre, mid, post, offs, out):
         identity = held.tile([P, P], F32, name="identity")
         make_identity(nc, identity[:])
 
-        def blocks_to_columns(rows, name):
-            blocks = rows.shape[0]
-            columns_ps = psum.tile([P, WIDE], F32, name="flipped_ps")
-            nc.tensor.matmul(columns_ps[:, 0:blocks], rows, identity[0:blocks, 0:blocks])
-            columns = held.tile([P, blocks], F32, name=name)
-            nc.scalar.activation(columns[:], columns_ps[:, 0:blocks], COPY)
-            return columns
-
-        def spread(columns, first):
-            spread_ps = spreads.tile([P, WIDE], F32, name="spread_ps")
-            for i in range(GROUP):
-                one = columns[:, first + i : first + i + 1]
-                nc.tensor.transpose(spread_ps[:, i * P : (i + 1) * P], one.to_broadcast([P, P]), identity[:])
-            return spread_ps
-
-        pre_cols = blocks_to_columns(pre_rows[:], "pre_cols")
+        columns_ps = products.tile([P, WIDE], F32, name="product_ps")
+        nc.tensor.transpose(columns_ps[:, 0 : 2 * blocks], rows[:], identity[0 : 2 * blocks, 0 : 2 * blocks])
+        columns = held.tile([P, 2 * blocks], F32, name="columns")
+        nc.scalar.activation(columns[:], columns_ps[:, 0 : 2 * blocks], COPY)
+        pre_cols, post_cols = columns[:, 0:blocks], columns[:, blocks : 2 * blocks]
 
         haar = held.tile([P, P], F32, name="haar")
         sums = identity
@@ -107,80 +113,95 @@ def tile_waveletlayer_kernel(tc, x, pre, mid, post, offs, out):
         w = held.tile([P, S], F32, name="w")
         flipped = {}
 
-        def flip_x(g):
+        def flip_x(first, width):
             flipped_ps = psum.tile([P, WIDE], F32, name="flipped_ps")
-            flipped[g] = ring.tile([P, WIDE], F32, name="flipped")
-            for i in range(GROUP):
-                b = g * GROUP + i
-                nc.tensor.transpose(flipped_ps[:, i * P : (i + 1) * P], x_sb[:, b * P : (b + 1) * P], identity[:])
-            for i in range(GROUP):
-                b = g * GROUP + i
-                nc.scalar.mul(flipped[g][:, i * P : (i + 1) * P], flipped_ps[:, i * P : (i + 1) * P], pre_cols[:, b : b + 1])
+            flipped[first] = ring.tile([P, WIDE], F32, name="flipped")
+            for i in range(0, width, P):
+                nc.tensor.transpose(flipped_ps[:, i : i + P], x_sb[:, first + i : first + i + P], identity[:])
+            for i in range(0, width, P):
+                b = (first + i) // P
+                nc.scalar.mul(flipped[first][:, i : i + P], flipped_ps[:, i : i + P], pre_cols[:, b : b + 1])
 
-        def analyse_on_tensor(g):
+        def analyse_on_tensor(first, width):
             product_ps = products.tile([P, WIDE], F32, name="product_ps")
-            for i in range(GROUP):
-                nc.tensor.matmul(product_ps[:, i * P : (i + 1) * P], flipped[g][:, i * P : (i + 1) * P], haar[:])
+            for i in range(0, width, P):
+                nc.tensor.matmul(product_ps[:, i : i + P], flipped[first][:, i : i + P], haar[:])
             for (in_block, count), in_w in zip(coefficient_places(P), coefficient_places(S)):
-                first = in_w[0] + g * GROUP * count
+                to = in_w[0] + first // P * count
                 nc.scalar.activation(
-                    grouped(w[:, first : first + GROUP * count], count),
-                    grouped(product_ps[:], P)[:, :, in_block : in_block + count],
+                    grouped(w[:, to : to + width // P * count], count),
+                    grouped(product_ps[:, 0:width], P)[:, :, in_block : in_block + count],
                     COPY,
                 )
 
-        sums = {k: held.tile([P, (S - split) >> k], F32, name=f"sum{k}") for k in (0, 1, 2, 3)}
-        diffs = {k: held.tile([P, (S - split) >> k], F32, name=f"diff{k}") for k in (1, 2, 3)}
+        a = {k: held.tile([P, (S - SPLIT) >> k], F32, name=f"a{k}") for k in (1, 2, 3)}
+        a_2_scaled = held.tile([P, (S - SPLIT) >> 2], F32, name="a_2_scaled")
+        d = {k: held.tile([P, (S - SPLIT) >> k], F32, name=f"d{k}") for k in (2, 3)}
+        y = {}
 
-        def scale(v):
-            pre_ps = spread(pre_cols, (IN_TENSOR + v) * GROUP)
+        def scale(first, width):
+            here = first - SPLIT
+            y[first] = scaled.tile([P, max(WIDE, rest)], F32, name="y")
             nc.vector.scalar_tensor_tensor(
-                across(sums[0][:, v * WIDE : (v + 1) * WIDE], 2),
-                grouped(x_sb[:, split + v * WIDE : split + (v + 1) * WIDE], 2),
-                R**4,
-                grouped(pre_ps[:], 2),
+                across(y[first][:, 0:width], 2),
+                grouped(x_sb[:, first : first + width], 2),
+                R,
+                grouped(pre_sb[:, here : here + width], 2),
                 MULT,
                 MULT,
             )
 
-        def halve(k, two_runs, sum_to, first):
+        def halve(two_runs, sum_to, difference_to):
             n = two_runs.shape[1] // 2
             even, odd = two_runs[:, 0:n], two_runs[:, n : 2 * n]
-            d_k = slice((S >> k) + first, (S >> k) + first + n)
-            if k < 4:
-                nc.vector.tensor_tensor(sum_to, grouped(even, 2), grouped(odd, 2), ADD)
-                here = slice(first - (split >> k), first - (split >> k) + n)
-                nc.vector.tensor_tensor(diffs[k][:, here], even, odd, SUB)
-                nc.scalar.mul(w[:, d_k], diffs[k][:, here], R ** (k - 4))
-            else:
-                nc.vector.tensor_tensor(w[:, first : first + n], even, odd, ADD)
-                nc.vector.tensor_tensor(w[:, d_k], even, odd, SUB)
+            nc.vector.tensor_tensor(sum_to, grouped(even, 2), grouped(odd, 2), ADD)
+            nc.vector.tensor_tensor(difference_to, even, odd, SUB)
 
-        def first_level(v):
-            halve(1, sums[0][:, v * WIDE : (v + 1) * WIDE], across(sums[1][:, v * WIDE // 2 : (v + 1) * WIDE // 2], 2), (split + v * WIDE) >> 1)
+        def a_1(first, width):
+            return a[1][:, (first - SPLIT) // 2 : (first - SPLIT + width) // 2]
 
-        def second_level(v):
-            rows = slice(v * WIDE // 8, (v + 1) * WIDE // 8)
-            halve(2, sums[1][:, v * WIDE // 2 : (v + 1) * WIDE // 2], across(sums[2][:], 2)[:, rows, :], (split + v * WIDE) >> 2)
+        def first_level(first, width):
+            d_1 = slice((S + first) // 2, (S + first + width) // 2)
+            halve(y[first][:, 0:width], across(a_1(first, width), 2), w[:, d_1])
 
-        for i in range(max(IN_TENSOR, in_vector) + 1):
-            if i < IN_TENSOR:
-                flip_x(i)
-            if i < in_vector:
-                scale(i)
-            if 0 < i <= IN_TENSOR:
-                analyse_on_tensor(i - 1)
-            if 0 < i <= in_vector:
-                second_level(i - 1)
-            if i < in_vector:
-                first_level(i)
-        halve(3, sums[2][:], across(sums[3][:], 2), split >> 3)
-        halve(4, sums[3][:], None, split >> 4)
+        def second_level(first, width):
+            here = first - SPLIT
+            rows = slice(here // 8, (here + width) // 8)
+            halve(a_1(first, width), across(a[2][:], 2)[:, rows, :], d[2][:, here // 4 : (here + width) // 4])
+
+        def vector_columns(k):
+            return slice((S + SPLIT) >> k, (2 * S) >> k)
+
+        for i in range(len(tensor_portions) + 1):
+            if i < len(tensor_portions):
+                flip_x(*tensor_portions[i])
+            if i > 0:
+                analyse_on_tensor(*tensor_portions[i - 1])
+            if i < len(vector_portions):
+                scale(*vector_portions[i])
+                first_level(*vector_portions[i])
+                second_level(*vector_portions[i])
+        nc.vector.tensor_scalar_mul(a_2_scaled[:], a[2][:], R**3)
+        nc.vector.tensor_scalar_mul(w[:, vector_columns(2)], d[2][:], R)
+        halve(a_2_scaled[:], across(a[3][:], 2), d[3][:])
+        nc.vector.tensor_scalar_mul(w[:, vector_columns(3)], d[3][:], 1 / R)
+        halve(a[3][:], w[:, SPLIT >> 4 : ROOT], w[:, vector_columns(4)])
 
         haar_t_ps = products.tile([P, WIDE], F32, name="product_ps")
         nc.tensor.transpose(haar_t_ps[:, 0:P], haar[:], identity[:])
         haar_t = held.tile([P, P], F32, name="haar_t")
         nc.scalar.activation(haar_t[:], haar_t_ps[:, 0:P], COPY)
+
+        folded = {}
+        for g in FOLDED:
+            diagonals = held.tile([P, WIDE], F32, name=f"diagonals{g}")
+            for i in range(GROUP):
+                b = g * GROUP + i
+                nc.scalar.mul(diagonals[:, i * P : (i + 1) * P], identity[:], post_cols[:, b : b + 1])
+            folded_ps = products.tile([P, WIDE], F32, name="product_ps")
+            nc.tensor.matmul(folded_ps[:], haar[:], diagonals[:])
+            folded[g] = held.tile([P, WIDE], F32, name=f"folded{g}")
+            nc.scalar.activation(folded[g][:], folded_ps[:], COPY)
 
         t = held.tile([P, N], F32, name="t")
 
@@ -220,9 +241,13 @@ def tile_waveletlayer_kernel(tc, x, pre, mid, post, offs, out):
         def synthesise_on_tensor(g):
             product_ps = products.tile([P, WIDE], F32, name="product_ps")
             for i in range(GROUP):
-                nc.tensor.matmul(product_ps[:, i * P : (i + 1) * P], flipped[g][:, i * P : (i + 1) * P], haar_t[:])
+                block = slice(i * P, (i + 1) * P)
+                nc.tensor.matmul(product_ps[:, block], flipped[g][:, block], folded[g][:, block] if g in folded else haar_t[:])
             cols = slice(g * WIDE, (g + 1) * WIDE)
-            nc.vector.tensor_tensor(o_sb[:, cols], product_ps[:], post_sb[:, cols], MULT)
+            if g in folded:
+                nc.scalar.activation(o_sb[:, cols], product_ps[:], COPY)
+            else:
+                nc.vector.tensor_tensor(o_sb[:, cols], product_ps[:], post_sb[:, cols], MULT)
             nc.sync.dma_start(out[:, cols], o_sb[:, cols])
 
         flip_t(OUT_TENSOR_ORDER[0])

@@ -21,10 +21,12 @@ SIGNS = ((0, 1.0), (1, -1.0))
 GROUP = 4
 WIDE = GROUP * P
 GROUPS = S // WIDE
-SPLIT = 18 * P
-OUT_TENSOR = 5
-OUT_TENSOR_ORDER = (2, 3, 1, 0, 4)
-FOLDED = OUT_TENSOR_ORDER[:2]
+SPLIT = S // 2
+OUT_SPLIT = 22 * P
+OUT_TENSOR = tuple((g * WIDE, WIDE) for g in (2, 3, 1, 0, 4)) + ((5 * WIDE, OUT_SPLIT - 5 * WIDE),)
+FOLDED = OUT_TENSOR[:2]
+OUT_HALF = (S - OUT_SPLIT) // 2
+OUT_VECTOR = ((OUT_SPLIT, OUT_HALF), (OUT_SPLIT + OUT_HALF, OUT_HALF))
 
 FLOPS = P * (2 * S + N + 4 * (S - ROOT))
 
@@ -46,16 +48,15 @@ def tile_waveletlayer_kernel(tc, x, pre, mid, post, offs, out):
     pre_row = pre.rearrange("o n -> (o n)")
     mid_row = mid.rearrange("o n -> (o n)")
     post_row = post.rearrange("o n -> (o n)")
-    tensor_portions = [(c, min(WIDE, SPLIT - c)) for c in range(0, SPLIT, WIDE)]
-    rest = (S - SPLIT - WIDE) // 2
-    vector_portions = [(SPLIT, WIDE), (SPLIT + WIDE, rest), (SPLIT + WIDE + rest, rest)]
+    tensor_portions = [(c, WIDE) for c in range(0, SPLIT, WIDE)]
+    vector_portions = [(c, WIDE) for c in range(SPLIT, S, WIDE)]
 
     with (
         tc.tile_pool(name="held", bufs=1) as held,
         tc.tile_pool(name="ring", bufs=3) as ring,
-        tc.tile_pool(name="scaled", bufs=1) as scaled,
         tc.psum_pool(name="psum", bufs=2) as psum,
         tc.psum_pool(name="products", bufs=3) as products,
+        tc.psum_pool(name="spreads", bufs=3) as spreads,
     ):
         offsets = held.tile([P, N // 16], U16, name="offsets")
         nc.sync.dma_start(offsets[:], offs)
@@ -64,24 +65,9 @@ def tile_waveletlayer_kernel(tc, x, pre, mid, post, offs, out):
         nc.sync.dma_start(rows[0:blocks, :], pre_row.rearrange("(b s) -> b s", s=P))
         nc.sync.dma_start(rows[blocks : 2 * blocks, :], post_row.rearrange("(b s) -> b s", s=P))
         x_sb = held.tile([P, S], F32, name="x_sb")
-        pre_sb = held.tile([P, S - SPLIT], F32, name="pre_sb")
-
-        def load_x(first, width):
-            nc.sync.dma_start(x_sb[:, first : first + width], x[:, first : first + width])
-
-        def load_pre_and_x(first, width):
-            here = first - SPLIT
-            nc.sync.dma_start(pre_sb[:, here : here + width], pre_row[first : first + width].partition_broadcast(P))
-            load_x(first, width)
-
-        load_x(*tensor_portions[0])
-        load_pre_and_x(*vector_portions[0])
-        load_x(*tensor_portions[1])
-        load_pre_and_x(*vector_portions[1])
-        load_x(*tensor_portions[2])
-        load_x(*tensor_portions[3])
-        load_pre_and_x(*vector_portions[2])
-        load_x(*tensor_portions[4])
+        for tensor_portion, vector_portion in zip(tensor_portions, vector_portions):
+            for first, width in (tensor_portion, vector_portion):
+                nc.sync.dma_start(x_sb[:, first : first + width], x[:, first : first + width])
         mid_sb = held.tile([P, N], F32, name="mid_sb")
         nc.sync.dma_start(mid_sb[:], mid_row.partition_broadcast(P))
         post_sb = held.tile([P, S], F32, name="post_sb")
@@ -92,11 +78,26 @@ def tile_waveletlayer_kernel(tc, x, pre, mid, post, offs, out):
         identity = held.tile([P, P], F32, name="identity")
         make_identity(nc, identity[:])
 
-        columns_ps = products.tile([P, WIDE], F32, name="product_ps")
+        is_even = held.tile([P, 1], F32, name="is_even")
+        nc.vector.tensor_reduce(is_even[:], grouped(identity[:], 2)[:, :, 0], mybir.AxisListType.X, ADD)
+        factors = held.tile([P, 1], F32, name="factors")
+        nc.vector.tensor_scalar(factors[:], is_even[:], R**4 - R, R, MULT, ADD)
+
+        columns_ps = psum.tile([P, WIDE], F32, name="flipped_ps")
         nc.tensor.transpose(columns_ps[:, 0 : 2 * blocks], rows[:], identity[0 : 2 * blocks, 0 : 2 * blocks])
-        columns = held.tile([P, 2 * blocks], F32, name="columns")
-        nc.scalar.activation(columns[:], columns_ps[:, 0 : 2 * blocks], COPY)
-        pre_cols, post_cols = columns[:, 0:blocks], columns[:, blocks : 2 * blocks]
+        pre_cols = held.tile([P, blocks], F32, name="pre_cols")
+        vector_blocks = slice(SPLIT // P, blocks)
+        nc.scalar.mul(pre_cols[:, vector_blocks], columns_ps[:, vector_blocks], factors[:])
+        nc.scalar.activation(pre_cols[:, 0 : SPLIT // P], columns_ps[:, 0 : SPLIT // P], COPY)
+        post_cols = held.tile([P, blocks], F32, name="post_cols")
+        nc.scalar.activation(post_cols[:], columns_ps[:, blocks : 2 * blocks], COPY)
+
+        def spread(first):
+            spread_ps = spreads.tile([P, WIDE], F32, name="spread_ps")
+            for i in range(0, WIDE, P):
+                b = (first + i) // P
+                nc.tensor.transpose(spread_ps[:, i : i + P], pre_cols[:, b : b + 1].to_broadcast([P, P]), identity[:])
+            return spread_ps
 
         haar = held.tile([P, P], F32, name="haar")
         sums = identity
@@ -134,58 +135,58 @@ def tile_waveletlayer_kernel(tc, x, pre, mid, post, offs, out):
                     COPY,
                 )
 
+        y = held.tile([P, S - SPLIT], F32, name="y")
         a = {k: held.tile([P, (S - SPLIT) >> k], F32, name=f"a{k}") for k in (1, 2, 3)}
-        a_2_scaled = held.tile([P, (S - SPLIT) >> 2], F32, name="a_2_scaled")
         d = {k: held.tile([P, (S - SPLIT) >> k], F32, name=f"d{k}") for k in (2, 3)}
-        y = {}
 
-        def scale(first, width):
-            here = first - SPLIT
-            y[first] = scaled.tile([P, max(WIDE, rest)], F32, name="y")
-            nc.vector.scalar_tensor_tensor(
-                across(y[first][:, 0:width], 2),
-                grouped(x_sb[:, first : first + width], 2),
-                R,
-                grouped(pre_sb[:, here : here + width], 2),
-                MULT,
+        def scale(first):
+            spread_ps = spread(first)
+            nc.vector.tensor_tensor(
+                across(y[:, first - SPLIT : first - SPLIT + WIDE], 2),
+                grouped(x_sb[:, first : first + WIDE], 2),
+                grouped(spread_ps[:], 2),
                 MULT,
             )
 
-        def halve(two_runs, sum_to, difference_to):
+        def runs_of(two_runs):
             n = two_runs.shape[1] // 2
-            even, odd = two_runs[:, 0:n], two_runs[:, n : 2 * n]
-            nc.vector.tensor_tensor(sum_to, grouped(even, 2), grouped(odd, 2), ADD)
-            nc.vector.tensor_tensor(difference_to, even, odd, SUB)
+            return two_runs[:, 0:n], two_runs[:, n : 2 * n]
 
-        def a_1(first, width):
-            return a[1][:, (first - SPLIT) // 2 : (first - SPLIT + width) // 2]
-
-        def first_level(first, width):
-            d_1 = slice((S + first) // 2, (S + first + width) // 2)
-            halve(y[first][:, 0:width], across(a_1(first, width), 2), w[:, d_1])
-
-        def second_level(first, width):
+        def first_level(first):
             here = first - SPLIT
-            rows = slice(here // 8, (here + width) // 8)
-            halve(a_1(first, width), across(a[2][:], 2)[:, rows, :], d[2][:, here // 4 : (here + width) // 4])
+            even, odd = runs_of(y[:, here : here + WIDE])
+            sum_to = across(a[1][:, here // 2 : (here + WIDE) // 2], 2)
+            nc.vector.scalar_tensor_tensor(sum_to, grouped(odd, 2), R**3, grouped(even, 2), MULT, ADD)
+            d_1 = slice((S + first) // 2, (S + first + WIDE) // 2)
+            nc.vector.scalar_tensor_tensor(w[:, d_1], even, R**-3, odd, MULT, SUB)
 
-        def vector_columns(k):
-            return slice((S + SPLIT) >> k, (2 * S) >> k)
+        def higher_level(k, two_runs, sum_to, here, n):
+            even, odd = runs_of(two_runs)
+            nc.vector.tensor_tensor(sum_to, grouped(even, 2), grouped(odd, 2), ADD)
+            nc.vector.tensor_tensor(d[k][:, here : here + n], even, odd, SUB)
+            to = ((S + SPLIT) >> k) + here
+            nc.scalar.mul(w[:, to : to + n], d[k][:, here : here + n], R ** (k - 4))
+
+        def second_level(first):
+            here = first - SPLIT
+            rows_8 = slice(here // 8, (here + WIDE) // 8)
+            higher_level(2, a[1][:, here // 2 : (here + WIDE) // 2], across(a[2][:], 2)[:, rows_8, :], here // 4, WIDE // 4)
 
         for i in range(len(tensor_portions) + 1):
             if i < len(tensor_portions):
                 flip_x(*tensor_portions[i])
+            if i < len(vector_portions):
+                scale(vector_portions[i][0])
             if i > 0:
                 analyse_on_tensor(*tensor_portions[i - 1])
+            if 0 < i <= len(vector_portions):
+                second_level(vector_portions[i - 1][0])
             if i < len(vector_portions):
-                scale(*vector_portions[i])
-                first_level(*vector_portions[i])
-                second_level(*vector_portions[i])
-        nc.vector.tensor_scalar_mul(a_2_scaled[:], a[2][:], R**3)
-        nc.vector.tensor_scalar_mul(w[:, vector_columns(2)], d[2][:], R)
-        halve(a_2_scaled[:], across(a[3][:], 2), d[3][:])
-        nc.vector.tensor_scalar_mul(w[:, vector_columns(3)], d[3][:], 1 / R)
-        halve(a[3][:], w[:, SPLIT >> 4 : ROOT], w[:, vector_columns(4)])
+                first_level(vector_portions[i][0])
+        higher_level(3, a[2][:], across(a[3][:], 2), 0, (S - SPLIT) >> 3)
+        even, odd = runs_of(a[3][:])
+        nc.vector.tensor_tensor(w[:, SPLIT >> 4 : ROOT], even, odd, ADD)
+        nc.vector.tensor_tensor(w[:, (S + SPLIT) >> 4 : (2 * S) >> 4], even, odd, SUB)
 
         haar_t_ps = products.tile([P, WIDE], F32, name="product_ps")
         nc.tensor.transpose(haar_t_ps[:, 0:P], haar[:], identity[:])
@@ -193,15 +194,15 @@ def tile_waveletlayer_kernel(tc, x, pre, mid, post, offs, out):
         nc.scalar.activation(haar_t[:], haar_t_ps[:, 0:P], COPY)
 
         folded = {}
-        for g in FOLDED:
-            diagonals = held.tile([P, WIDE], F32, name=f"diagonals{g}")
-            for i in range(GROUP):
-                b = g * GROUP + i
-                nc.scalar.mul(diagonals[:, i * P : (i + 1) * P], identity[:], post_cols[:, b : b + 1])
+        for first, width in FOLDED:
+            diagonals = held.tile([P, width], F32, name=f"diagonals{first}")
+            for i in range(0, width, P):
+                b = (first + i) // P
+                nc.scalar.mul(diagonals[:, i : i + P], identity[:], post_cols[:, b : b + 1])
             folded_ps = products.tile([P, WIDE], F32, name="product_ps")
-            nc.tensor.matmul(folded_ps[:], haar[:], diagonals[:])
-            folded[g] = held.tile([P, WIDE], F32, name=f"folded{g}")
-            nc.scalar.activation(folded[g][:], folded_ps[:], COPY)
+            nc.tensor.matmul(folded_ps[:, 0:width], haar[:], diagonals[:])
+            folded[first] = held.tile([P, width], F32, name=f"folded{first}")
+            nc.scalar.activation(folded[first][:], folded_ps[:, 0:width], COPY)
 
         t = held.tile([P, N], F32, name="t")
 
@@ -223,38 +224,38 @@ def tile_waveletlayer_kernel(tc, x, pre, mid, post, offs, out):
 
         o_sb = held.tile([P, S], F32, name="o_sb")
 
-        def flip_t(g):
+        def flip_t(first, width):
             packed = ring.tile([P, WIDE], F32, name="packed")
             for k, (in_block, count) in enumerate(coefficient_places(P)):
-                first = T_START[k] + g * GROUP * count
+                at = T_START[k] + first // P * count
                 nc.scalar.activation(
-                    grouped(packed[:], P)[:, :, in_block : in_block + count],
-                    grouped(t[:, first : first + GROUP * count], count),
+                    grouped(packed[:, 0:width], P)[:, :, in_block : in_block + count],
+                    grouped(t[:, at : at + width // P * count], count),
                     COPY,
                 )
             flipped_ps = psum.tile([P, WIDE], F32, name="flipped_ps")
-            for i in range(GROUP):
-                nc.tensor.transpose(flipped_ps[:, i * P : (i + 1) * P], packed[:, i * P : (i + 1) * P], identity[:])
-            flipped[g] = ring.tile([P, WIDE], F32, name="flipped")
-            nc.scalar.activation(flipped[g][:], flipped_ps[:], COPY)
+            for i in range(0, width, P):
+                nc.tensor.transpose(flipped_ps[:, i : i + P], packed[:, i : i + P], identity[:])
+            flipped[first] = ring.tile([P, WIDE], F32, name="flipped")
+            nc.scalar.activation(flipped[first][:, 0:width], flipped_ps[:, 0:width], COPY)
 
-        def synthesise_on_tensor(g):
+        def synthesise_on_tensor(first, width):
             product_ps = products.tile([P, WIDE], F32, name="product_ps")
-            for i in range(GROUP):
-                block = slice(i * P, (i + 1) * P)
-                nc.tensor.matmul(product_ps[:, block], flipped[g][:, block], folded[g][:, block] if g in folded else haar_t[:])
-            cols = slice(g * WIDE, (g + 1) * WIDE)
-            if g in folded:
-                nc.scalar.activation(o_sb[:, cols], product_ps[:], COPY)
+            for i in range(0, width, P):
+                matrix = folded[first][:, i : i + P] if first in folded else haar_t[:]
+                nc.tensor.matmul(product_ps[:, i : i + P], flipped[first][:, i : i + P], matrix)
+            cols = slice(first, first + width)
+            if first in folded:
+                nc.scalar.activation(o_sb[:, cols], product_ps[:, 0:width], COPY)
             else:
-                nc.vector.tensor_tensor(o_sb[:, cols], product_ps[:], post_sb[:, cols], MULT)
+                nc.vector.tensor_tensor(o_sb[:, cols], product_ps[:, 0:width], post_sb[:, cols], MULT)
             nc.sync.dma_start(out[:, cols], o_sb[:, cols])
 
-        flip_t(OUT_TENSOR_ORDER[0])
-        for g, next_g in zip(OUT_TENSOR_ORDER, OUT_TENSOR_ORDER[1:] + (None,)):
-            if next_g is not None:
-                flip_t(next_g)
-            synthesise_on_tensor(g)
+        flip_t(*OUT_TENSOR[0])
+        for portion, following in zip(OUT_TENSOR, OUT_TENSOR[1:] + (None,)):
+            if following is not None:
+                flip_t(*following)
+            synthesise_on_tensor(*portion)
 
         halves = {k: held.tile([P, ROOT << k], F32, name=f"halves{k}") for k in (1, 2, 3, 4)}
 
@@ -276,11 +277,11 @@ def tile_waveletlayer_kernel(tc, x, pre, mid, post, offs, out):
                         ADD,
                     )
 
-        def finish(g):
-            cols = slice(g * WIDE, (g + 1) * WIDE)
+        def finish(first, width):
+            cols = slice(first, first + width)
             nc.vector.scalar_tensor_tensor(
                 grouped(o_sb[:, cols], 2),
-                across(halves[4], 2)[:, g * WIDE // 2 : (g + 1) * WIDE // 2, :],
+                across(halves[4], 2)[:, first // 2 : (first + width) // 2, :],
                 R**4,
                 grouped(post_sb[:, cols], 2),
                 MULT,
@@ -288,14 +289,13 @@ def tile_waveletlayer_kernel(tc, x, pre, mid, post, offs, out):
             )
             nc.sync.dma_start(out[:, cols], o_sb[:, cols])
 
-        roots = WIDE // 16
-        double(1, OUT_TENSOR * roots, ROOT)
-        double(2, OUT_TENSOR * roots, ROOT)
-        for step in range(OUT_TENSOR, GROUPS + 2):
+        double(1, OUT_SPLIT // 16, ROOT)
+        double(2, OUT_SPLIT // 16, ROOT)
+        for step in range(len(OUT_VECTOR) + 2):
             for behind in range(3):
-                g = step - behind
-                if OUT_TENSOR <= g < GROUPS:
+                if 0 <= step - behind < len(OUT_VECTOR):
+                    first, width = OUT_VECTOR[step - behind]
                     if behind < 2:
-                        double(3 + behind, g * roots, (g + 1) * roots)
+                        double(3 + behind, first // 16, (first + width) // 16)
                     else:
-                        finish(g)
+                        finish(first, width)

@@ -69,10 +69,11 @@ def tile_waveletlayer_kernel(tc, x, pre, mid, post, offs, out):
             for first, width in (tensor_portion, vector_portion):
                 nc.sync.dma_start(x_sb[:, first : first + width], x[:, first : first + width])
         mid_sb = held.tile([P, N], F32, name="mid_sb")
-        nc.sync.dma_start(mid_sb[:], mid_row.partition_broadcast(P))
+        for first, last in ((768, 1280), (0, 256), (2048, N), (256, 768), (1280, 2048)):
+            nc.sync.dma_start(mid_sb[:, first:last], mid_row[first:last].partition_broadcast(P))
         post_sb = held.tile([P, S], F32, name="post_sb")
-        for g in range(0, GROUPS, 2):
-            cols = slice(g * WIDE, (g + 2) * WIDE)
+        for first, width in OUT_VECTOR + OUT_TENSOR[len(FOLDED) :]:
+            cols = slice(first, first + width)
             nc.sync.dma_start(post_sb[:, cols], post_row[cols].partition_broadcast(P))
 
         identity = held.tile([P, P], F32, name="identity")

@@ -23,8 +23,10 @@ WIDE = GROUP * P
 GROUPS = S // WIDE
 SPLIT = S // 2
 OUT_SPLIT = 22 * P
-OUT_TENSOR = tuple((g * WIDE, WIDE) for g in (2, 3, 1, 0, 4)) + ((5 * WIDE, OUT_SPLIT - 5 * WIDE),)
-FOLDED = OUT_TENSOR[:2]
+OUT_TENSOR = ((2 * WIDE, WIDE // 2), (2 * WIDE + WIDE // 2, WIDE // 2)) + tuple(
+    (g * WIDE, min(WIDE, OUT_SPLIT - g * WIDE)) for g in (3, 1, 0, 4, 5)
+)
+FOLDED = OUT_TENSOR[:3]
 OUT_HALF = (S - OUT_SPLIT) // 2
 OUT_VECTOR = ((OUT_SPLIT, OUT_HALF), (OUT_SPLIT + OUT_HALF, OUT_HALF))
 
@@ -195,7 +197,7 @@ def tile_waveletlayer_kernel(tc, x, pre, mid, post, offs, out):
         nc.scalar.activation(haar_t[:], haar_t_ps[:, 0:P], COPY)
 
         folded = {}
-        for first, width in FOLDED:
+        for first, width in FOLDED[2:] + FOLDED[:2]:
             diagonals = held.tile([P, width], F32, name=f"diagonals{first}")
             for i in range(0, width, P):
                 b = (first + i) // P
@@ -213,15 +215,39 @@ def tile_waveletlayer_kernel(tc, x, pre, mid, post, offs, out):
             )
 
         half = ROOT // 2
-        look_up(768, 1024)
+        look_up(768, 896)
         look_up(0, half)
         look_up(2048, 2048 + half)
         look_up(1152, 1280)
-        look_up(1024, 1152)
+        look_up(896, 1152)
         look_up(256, 768)
         look_up(half, ROOT)
         look_up(2048 + half, N)
-        look_up(1280, 2048)
+        look_up(1280, 1536)
+
+        halves = {k: held.tile([P, ROOT << k], F32, name=f"halves{k}") for k in (1, 2, 3, 4)}
+
+        def double(k, m0, m1):
+            g = 1 << (k - 1)
+            n = ROOT * g
+            f_k = t[:, T_START[k] + g * m0 : T_START[k] + g * m1]
+            for s, sign in SIGNS:
+                run = halves[k][:, s * n + g * m0 : s * n + g * m1]
+                if k == 1:
+                    nc.vector.scalar_tensor_tensor(run, f_k, sign, t[:, m0:m1], MULT, ADD)
+                else:
+                    nc.vector.scalar_tensor_tensor(
+                        grouped(run, 2),
+                        grouped(f_k, 2),
+                        sign * R ** (1 - k),
+                        across(halves[k - 1], 2)[:, g * m0 // 2 : g * m1 // 2, :],
+                        MULT,
+                        ADD,
+                    )
+
+        double(1, OUT_SPLIT // 16, ROOT)
+        look_up(1536, 2048)
+        double(2, OUT_SPLIT // 16, ROOT)
 
         o_sb = held.tile([P, S], F32, name="o_sb")
 
@@ -258,26 +284,6 @@ def tile_waveletlayer_kernel(tc, x, pre, mid, post, offs, out):
                 flip_t(*following)
             synthesise_on_tensor(*portion)
 
-        halves = {k: held.tile([P, ROOT << k], F32, name=f"halves{k}") for k in (1, 2, 3, 4)}
-
-        def double(k, m0, m1):
-            g = 1 << (k - 1)
-            n = ROOT * g
-            f_k = t[:, T_START[k] + g * m0 : T_START[k] + g * m1]
-            for s, sign in SIGNS:
-                run = halves[k][:, s * n + g * m0 : s * n + g * m1]
-                if k == 1:
-                    nc.vector.scalar_tensor_tensor(run, f_k, sign, t[:, m0:m1], MULT, ADD)
-                else:
-                    nc.vector.scalar_tensor_tensor(
-                        grouped(run, 2),
-                        grouped(f_k, 2),
-                        sign * R ** (1 - k),
-                        across(halves[k - 1], 2)[:, g * m0 // 2 : g * m1 // 2, :],
-                        MULT,
-                        ADD,
-                    )
-
         def finish(first, width):
             cols = slice(first, first + width)
             nc.vector.scalar_tensor_tensor(
@@ -290,8 +296,6 @@ def tile_waveletlayer_kernel(tc, x, pre, mid, post, offs, out):
             )
             nc.sync.dma_start(out[:, cols], o_sb[:, cols])
 
-        double(1, OUT_SPLIT // 16, ROOT)
-        double(2, OUT_SPLIT // 16, ROOT)
         for step in range(len(OUT_VECTOR) + 2):
             for behind in range(3):
                 if 0 <= step - behind < len(OUT_VECTOR):

@@ -60,8 +60,6 @@ def tile_waveletlayer_kernel(tc, x, pre, mid, post, offs, out):
         tc.psum_pool(name="products", bufs=3) as products,
         tc.psum_pool(name="spreads", bufs=3) as spreads,
     ):
-        offsets = held.tile([P, N // 16], U16, name="offsets")
-        nc.sync.dma_start(offsets[:], offs)
         blocks = S // P
         rows = held.tile([2 * blocks, P], F32, name="rows")
         nc.sync.dma_start(rows[0:blocks, :], pre_row.rearrange("(b s) -> b s", s=P))
@@ -70,6 +68,8 @@ def tile_waveletlayer_kernel(tc, x, pre, mid, post, offs, out):
         for tensor_portion, vector_portion in zip(tensor_portions, vector_portions):
             for first, width in (tensor_portion, vector_portion):
                 nc.sync.dma_start(x_sb[:, first : first + width], x[:, first : first + width])
+        offsets = held.tile([P, N // 16], U16, name="offsets")
+        nc.sync.dma_start(offsets[:], offs)
         mid_sb = held.tile([P, N], F32, name="mid_sb")
         for first, last in ((768, 1280), (0, 256), (2048, N), (256, 768), (1280, 2048)):
             nc.sync.dma_start(mid_sb[:, first:last], mid_row[first:last].partition_broadcast(P))
@@ -130,12 +130,20 @@ def tile_waveletlayer_kernel(tc, x, pre, mid, post, offs, out):
             product_ps = products.tile([P, WIDE], F32, name="product_ps")
             for i in range(0, width, P):
                 nc.tensor.matmul(product_ps[:, i : i + P], flipped[first][:, i : i + P], haar[:])
-            for (in_block, count), in_w in zip(coefficient_places(P), coefficient_places(S)):
+            product = grouped(product_ps[:, 0:width], P)
+            count = P >> 4
+            to = first // P * count
+            nc.scalar.activation(
+                w[:, 0 : 2 * ROOT].rearrange("p (h n) -> p h n", h=2)[:, :, to : to + width // P * count].rearrange(
+                    "p h (b c) -> p h b c", c=count
+                ),
+                product[:, :, 0 : 2 * count].rearrange("p b (h c) -> p h b c", h=2),
+                COPY,
+            )
+            for (in_block, count), in_w in list(zip(coefficient_places(P), coefficient_places(S)))[2:]:
                 to = in_w[0] + first // P * count
                 nc.scalar.activation(
-                    grouped(w[:, to : to + width // P * count], count),
-                    grouped(product_ps[:, 0:width], P)[:, :, in_block : in_block + count],
-                    COPY,
+                    grouped(w[:, to : to + width // P * count], count), product[:, :, in_block : in_block + count], COPY
                 )
 
         y = held.tile([P, S - SPLIT], F32, name="y")
@@ -168,7 +176,10 @@ def tile_waveletlayer_kernel(tc, x, pre, mid, post, offs, out):
             nc.vector.tensor_tensor(sum_to, grouped(even, 2), grouped(odd, 2), ADD)
             nc.vector.tensor_tensor(d[k][:, here : here + n], even, odd, SUB)
             to = ((S + SPLIT) >> k) + here
-            nc.scalar.mul(w[:, to : to + n], d[k][:, here : here + n], R ** (k - 4))
+            if k == 2:
+                nc.scalar.mul(w[:, to : to + n], d[k][:, here : here + n], R ** (k - 4))
+            else:
+                nc.vector.tensor_scalar_mul(w[:, to : to + n], d[k][:, here : here + n], R ** (k - 4))
 
         def second_level(first):
             here = first - SPLIT
@@ -251,18 +262,23 @@ def tile_waveletlayer_kernel(tc, x, pre, mid, post, offs, out):
 
         o_sb = held.tile([P, S], F32, name="o_sb")
 
+        packed = held.tile([P, OUT_SPLIT], F32, name="packed")
+
+        def pack(k, first, width):
+            in_block, count = coefficient_places(P)[k]
+            at = T_START[k] + first // P * count
+            nc.scalar.activation(
+                grouped(packed[:, first : first + width], P)[:, :, in_block : in_block + count],
+                grouped(t[:, at : at + width // P * count], count),
+                COPY,
+            )
+
         def flip_t(first, width):
-            packed = ring.tile([P, WIDE], F32, name="packed")
-            for k, (in_block, count) in enumerate(coefficient_places(P)):
-                at = T_START[k] + first // P * count
-                nc.scalar.activation(
-                    grouped(packed[:, 0:width], P)[:, :, in_block : in_block + count],
-                    grouped(t[:, at : at + width // P * count], count),
-                    COPY,
-                )
+            pack(3, first, width)
+            pack(4, first, width)
             flipped_ps = psum.tile([P, WIDE], F32, name="flipped_ps")
             for i in range(0, width, P):
-                nc.tensor.transpose(flipped_ps[:, i : i + P], packed[:, i : i + P], identity[:])
+                nc.tensor.transpose(flipped_ps[:, i : i + P], packed[:, first + i : first + i + P], identity[:])
             flipped[first] = ring.tile([P, WIDE], F32, name="flipped")
             nc.scalar.activation(flipped[first][:, 0:width], flipped_ps[:, 0:width], COPY)
 
@@ -278,9 +294,17 @@ def tile_waveletlayer_kernel(tc, x, pre, mid, post, offs, out):
                 nc.vector.tensor_tensor(o_sb[:, cols], product_ps[:, 0:width], post_sb[:, cols], MULT)
             nc.sync.dma_start(out[:, cols], o_sb[:, cols])
 
+        pack(0, 0, 4 * WIDE)
+        pack(1, 0, 4 * WIDE)
+        pack(2, 2 * WIDE, 2 * WIDE)
         flip_t(*OUT_TENSOR[0])
         for portion, following in zip(OUT_TENSOR, OUT_TENSOR[1:] + (None,)):
             if following is not None:
+                if following[0] == 1 * WIDE:
+                    pack(2, 0, 2 * WIDE)
+                elif following[0] == 4 * WIDE:
+                    for k in (0, 1, 2):
+                        pack(k, 4 * WIDE, OUT_SPLIT - 4 * WIDE)
                 flip_t(*following)
             synthesise_on_tensor(*portion)
 

import math

import concourse.mybir as mybir
from concourse.masks import make_identity

F32 = mybir.dt.float32
U16 = mybir.dt.uint16
ADD = mybir.AluOpType.add
SUB = mybir.AluOpType.subtract
MULT = mybir.AluOpType.mult
COPY = mybir.ActivationFunctionType.Copy

P = 128
S = 4096
N = 2304
R = math.sqrt(0.5)
ROOT = S // 16
T_START = {0: 0, 1: 2048, 2: 1024, 3: 512, 4: 256}
SIGNS = ((0, 1.0), (1, -1.0))

GROUP = 4
WIDE = GROUP * P
GROUPS = S // WIDE
SPLIT = S // 2
OUT_SPLIT = 22 * P
OUT_TENSOR = ((2 * WIDE, WIDE // 2), (2 * WIDE + WIDE // 2, WIDE // 2)) + tuple(
    (g * WIDE, min(WIDE, OUT_SPLIT - g * WIDE)) for g in (3, 1, 0, 4, 5)
)
FOLDED = OUT_TENSOR[:3]
OUT_HALF = (S - OUT_SPLIT) // 2
OUT_VECTOR = ((OUT_SPLIT, OUT_HALF), (OUT_SPLIT + OUT_HALF, OUT_HALF))

FLOPS = P * (2 * S + N + 4 * (S - ROOT))


def grouped(ap, g):
    return ap.rearrange("p (j r) -> p j r", r=g)


def across(ap, runs):
    return ap.rearrange("p (r j) -> p j r", r=runs)


def coefficient_places(n):
    return [(0, n >> 4)] + [(n >> k, n >> k) for k in (4, 3, 2, 1)]


def tile_waveletlayer_kernel(tc, x, pre, mid, post, offs, out):
    nc = tc.nc
    pre_row = pre.rearrange("o n -> (o n)")
    mid_row = mid.rearrange("o n -> (o n)")
    post_row = post.rearrange("o n -> (o n)")
    tensor_portions = [(c, WIDE) for c in range(0, SPLIT, WIDE)]
    vector_portions = [(c, WIDE) for c in range(SPLIT, S, WIDE)]

    with (
        tc.tile_pool(name="held", bufs=1) as held,
        tc.tile_pool(name="ring", bufs=3) as ring,
        tc.psum_pool(name="psum", bufs=2) as psum,
        tc.psum_pool(name="products", bufs=3) as products,
        tc.psum_pool(name="spreads", bufs=3) as spreads,
    ):
        blocks = S // P
        rows = held.tile([2 * blocks, P], F32, name="rows")
        nc.sync.dma_start(rows[0:blocks, :], pre_row.rearrange("(b s) -> b s", s=P))
        nc.sync.dma_start(rows[blocks : 2 * blocks, :], post_row.rearrange("(b s) -> b s", s=P))
        x_sb = held.tile([P, S], F32, name="x_sb")
        for tensor_portion, vector_portion in zip(tensor_portions, vector_portions):
            for first, width in (tensor_portion, vector_portion):
                nc.sync.dma_start(x_sb[:, first : first + width], x[:, first : first + width])
        offsets = held.tile([P, N // 16], U16, name="offsets")
        nc.sync.dma_start(offsets[:], offs)
        mid_sb = held.tile([P, N], F32, name="mid_sb")
        for first, last in ((768, 1280), (0, 256), (2048, N), (256, 768), (1280, 2048)):
            nc.sync.dma_start(mid_sb[:, first:last], mid_row[first:last].partition_broadcast(P))
        post_sb = held.tile([P, S], F32, name="post_sb")
        for first, width in OUT_VECTOR + OUT_TENSOR[len(FOLDED) :]:
            cols = slice(first, first + width)
            nc.sync.dma_start(post_sb[:, cols], post_row[cols].partition_broadcast(P))

        identity = held.tile([P, P], F32, name="identity")
        make_identity(nc, identity[:])

        is_even = held.tile([P, 1], F32, name="is_even")
        nc.vector.tensor_reduce(is_even[:], grouped(identity[:], 2)[:, :, 0], mybir.AxisListType.X, ADD)
        factors = held.tile([P, 1], F32, name="factors")
        nc.vector.tensor_scalar(factors[:], is_even[:], R**4 - R, R, MULT, ADD)

        columns_ps = psum.tile([P, WIDE], F32, name="flipped_ps")
        nc.tensor.transpose(columns_ps[:, 0 : 2 * blocks], rows[:], identity[0 : 2 * blocks, 0 : 2 * blocks])
        pre_cols = held.tile([P, blocks], F32, name="pre_cols")
        vector_blocks = slice(SPLIT // P, blocks)
        nc.scalar.mul(pre_cols[:, vector_blocks], columns_ps[:, vector_blocks], factors[:])
        nc.scalar.activation(pre_cols[:, 0 : SPLIT // P], columns_ps[:, 0 : SPLIT // P], COPY)
        post_cols = held.tile([P, blocks], F32, name="post_cols")
        nc.scalar.activation(post_cols[:], columns_ps[:, blocks : 2 * blocks], COPY)

        def spread(first):
            spread_ps = spreads.tile([P, WIDE], F32, name="spread_ps")
            for i in range(0, WIDE, P):
                b = (first + i) // P
                nc.tensor.transpose(spread_ps[:, i : i + P], pre_cols[:, b : b + 1].to_broadcast([P, P]), identity[:])
            return spread_ps

        haar = held.tile([P, P], F32, name="haar")
        sums = identity
        for k in (1, 2, 3, 4):
            half = P >> k
            two = grouped(sums[:], 2)
            sums = held.tile([P, half], F32, name=f"impulse_sum{k}")
            nc.gpsimd.tensor_tensor(sums[:], two[:, :, 0], two[:, :, 1], ADD)
            diff = held.tile([P, half], F32, name=f"impulse_diff{k}")
            nc.gpsimd.tensor_tensor(diff[:], two[:, :, 0], two[:, :, 1], SUB)
            nc.scalar.mul(haar[:, half : 2 * half], diff[:], R**k)
        nc.scalar.mul(haar[:, 0 : P >> 4], sums[:], R**4)

        w = held.tile([P, S], F32, name="w")
        flipped = {}

        def flip_x(first, width):
            flipped_ps = psum.tile([P, WIDE], F32, name="flipped_ps")
            flipped[first] = ring.tile([P, WIDE], F32, name="flipped")
            for i in range(0, width, P):
                nc.tensor.transpose(flipped_ps[:, i : i + P], x_sb[:, first + i : first + i + P], identity[:])
            for i in range(0, width, P):
                b = (first + i) // P
                nc.scalar.mul(flipped[first][:, i : i + P], flipped_ps[:, i : i + P], pre_cols[:, b : b + 1])

        def analyse_on_tensor(first, width):
            product_ps = products.tile([P, WIDE], F32, name="product_ps")
            for i in range(0, width, P):
                nc.tensor.matmul(product_ps[:, i : i + P], flipped[first][:, i : i + P], haar[:])
            product = grouped(product_ps[:, 0:width], P)
            count = P >> 4
            to = first // P * count
            nc.scalar.activation(
                w[:, 0 : 2 * ROOT].rearrange("p (h n) -> p h n", h=2)[:, :, to : to + width // P * count].rearrange(
                    "p h (b c) -> p h b c", c=count
                ),
                product[:, :, 0 : 2 * count].rearrange("p b (h c) -> p h b c", h=2),
                COPY,
            )
            for (in_block, count), in_w in list(zip(coefficient_places(P), coefficient_places(S)))[2:]:
                to = in_w[0] + first // P * count
                nc.scalar.activation(
                    grouped(w[:, to : to + width // P * count], count), product[:, :, in_block : in_block + count], COPY
                )

        y = held.tile([P, S - SPLIT], F32, name="y")
        a = {k: held.tile([P, (S - SPLIT) >> k], F32, name=f"a{k}") for k in (1, 2, 3)}
        d = {k: held.tile([P, (S - SPLIT) >> k], F32, name=f"d{k}") for k in (2, 3)}

        def scale(first):
            spread_ps = spread(first)
            nc.vector.tensor_tensor(
                across(y[:, first - SPLIT : first - SPLIT + WIDE], 2),
                grouped(x_sb[:, first : first + WIDE], 2),
                grouped(spread_ps[:], 2),
                MULT,
            )

        def runs_of(two_runs):
            n = two_runs.shape[1] // 2
            return two_runs[:, 0:n], two_runs[:, n : 2 * n]

        def first_level(first):
            here = first - SPLIT
            even, odd = runs_of(y[:, here : here + WIDE])
            sum_to = across(a[1][:, here // 2 : (here + WIDE) // 2], 2)
            nc.vector.scalar_tensor_tensor(sum_to, grouped(odd, 2), R**3, grouped(even, 2), MULT, ADD)
            d_1 = slice((S + first) // 2, (S + first + WIDE) // 2)
            nc.vector.scalar_tensor_tensor(w[:, d_1], even, R**-3, odd, MULT, SUB)

        def higher_level(k, two_runs, sum_to, here, n):
            even, odd = runs_of(two_runs)
            nc.vector.tensor_tensor(sum_to, grouped(even, 2), grouped(odd, 2), ADD)
            nc.vector.tensor_tensor(d[k][:, here : here + n], even, odd, SUB)
            to = ((S + SPLIT) >> k) + here
            if k == 2:
                nc.scalar.mul(w[:, to : to + n], d[k][:, here : here + n], R ** (k - 4))
            else:
                nc.vector.tensor_scalar_mul(w[:, to : to + n], d[k][:, here : here + n], R ** (k - 4))

        def second_level(first):
            here = first - SPLIT
            rows_8 = slice(here // 8, (here + WIDE) // 8)
            higher_level(2, a[1][:, here // 2 : (here + WIDE) // 2], across(a[2][:], 2)[:, rows_8, :], here // 4, WIDE // 4)

        for i in range(len(tensor_portions) + 1):
            if i < len(tensor_portions):
                flip_x(*tensor_portions[i])
            if i < len(vector_portions):
                scale(vector_portions[i][0])
            if i > 0:
                analyse_on_tensor(*tensor_portions[i - 1])
            if 0 < i <= len(vector_portions):
                second_level(vector_portions[i - 1][0])
            if i < len(vector_portions):
                first_level(vector_portions[i][0])
        higher_level(3, a[2][:], across(a[3][:], 2), 0, (S - SPLIT) >> 3)
        even, odd = runs_of(a[3][:])
        nc.vector.tensor_tensor(w[:, SPLIT >> 4 : ROOT], even, odd, ADD)
        nc.vector.tensor_tensor(w[:, (S + SPLIT) >> 4 : (2 * S) >> 4], even, odd, SUB)

        haar_t_ps = products.tile([P, WIDE], F32, name="product_ps")
        nc.tensor.transpose(haar_t_ps[:, 0:P], haar[:], identity[:])
        haar_t = held.tile([P, P], F32, name="haar_t")
        nc.scalar.activation(haar_t[:], haar_t_ps[:, 0:P], COPY)

        folded = {}
        for first, width in FOLDED[2:] + FOLDED[:2]:
            diagonals = held.tile([P, width], F32, name=f"diagonals{first}")
            for i in range(0, width, P):
                b = (first + i) // P
                nc.scalar.mul(diagonals[:, i : i + P], identity[:], post_cols[:, b : b + 1])
            folded_ps = products.tile([P, WIDE], F32, name="product_ps")
            nc.tensor.matmul(folded_ps[:, 0:width], haar[:], diagonals[:])
            folded[first] = held.tile([P, width], F32, name=f"folded{first}")
            nc.scalar.activation(folded[first][:], folded_ps[:, 0:width], COPY)

        t = held.tile([P, N], F32, name="t")

        def look_up(first, last):
            nc.vector.tensor_tensor(
                t[:, first:last], w[:].indirect(offsets[:, first // 16 : last // 16]), mid_sb[:, first:last], MULT
            )

        half = ROOT // 2
        look_up(768, 896)
        look_up(0, half)
        look_up(2048, 2048 + half)
        look_up(1152, 1280)
        look_up(896, 1152)
        look_up(256, 768)
        look_up(half, ROOT)
        look_up(2048 + half, N)
        look_up(1280, 1536)

        halves = {k: held.tile([P, ROOT << k], F32, name=f"halves{k}") for k in (1, 2, 3, 4)}

        def double(k, m0, m1):
            g = 1 << (k - 1)
            n = ROOT * g
            f_k = t[:, T_START[k] + g * m0 : T_START[k] + g * m1]
            for s, sign in SIGNS:
                run = halves[k][:, s * n + g * m0 : s * n + g * m1]
                if k == 1:
                    nc.vector.scalar_tensor_tensor(run, f_k, sign, t[:, m0:m1], MULT, ADD)
                else:
                    nc.vector.scalar_tensor_tensor(
                        grouped(run, 2),
                        grouped(f_k, 2),
                        sign * R ** (1 - k),
                        across(halves[k - 1], 2)[:, g * m0 // 2 : g * m1 // 2, :],
                        MULT,
                        ADD,
                    )

        double(1, OUT_SPLIT // 16, ROOT)
        look_up(1536, 2048)
        double(2, OUT_SPLIT // 16, ROOT)

        o_sb = held.tile([P, S], F32, name="o_sb")

        packed = held.tile([P, OUT_SPLIT], F32, name="packed")

        def pack(k, first, width):
            in_block, count = coefficient_places(P)[k]
            at = T_START[k] + first // P * count
            nc.scalar.activation(
                grouped(packed[:, first : first + width], P)[:, :, in_block : in_block + count],
                grouped(t[:, at : at + width // P * count], count),
                COPY,
            )

        def flip_t(first, width):
            pack(3, first, width)
            pack(4, first, width)
            flipped_ps = psum.tile([P, WIDE], F32, name="flipped_ps")
            for i in range(0, width, P):
                nc.tensor.transpose(flipped_ps[:, i : i + P], packed[:, first + i : first + i + P], identity[:])
            flipped[first] = ring.tile([P, WIDE], F32, name="flipped")
            nc.scalar.activation(flipped[first][:, 0:width], flipped_ps[:, 0:width], COPY)

        def synthesise_on_tensor(first, width):
            product_ps = products.tile([P, WIDE], F32, name="product_ps")
            for i in range(0, width, P):
                matrix = folded[first][:, i : i + P] if first in folded else haar_t[:]
                nc.tensor.matmul(product_ps[:, i : i + P], flipped[first][:, i : i + P], matrix)
            cols = slice(first, first + width)
            if first in folded:
                nc.scalar.activation(o_sb[:, cols], product_ps[:, 0:width], COPY)
            else:
                nc.vector.tensor_tensor(o_sb[:, cols], product_ps[:, 0:width], post_sb[:, cols], MULT)
            nc.sync.dma_start(out[:, cols], o_sb[:, cols])

        pack(0, 0, 4 * WIDE)
        pack(1, 0, 4 * WIDE)
        pack(2, 2 * WIDE, 2 * WIDE)
        flip_t(*OUT_TENSOR[0])
        for portion, following in zip(OUT_TENSOR, OUT_TENSOR[1:] + (None,)):
            if following is not None:
                if following[0] == 1 * WIDE:
                    pack(2, 0, 2 * WIDE)
                elif following[0] == 4 * WIDE:
                    for k in (0, 1, 2):
                        pack(k, 4 * WIDE, OUT_SPLIT - 4 * WIDE)
                flip_t(*following)
            synthesise_on_tensor(*portion)

        def finish(first, width):
            cols = slice(first, first + width)
            nc.vector.scalar_tensor_tensor(
                grouped(o_sb[:, cols], 2),
                across(halves[4], 2)[:, first // 2 : (first + width) // 2, :],
                R**4,
                grouped(post_sb[:, cols], 2),
                MULT,
                MULT,
            )
            nc.sync.dma_start(out[:, cols], o_sb[:, cols])

        for step in range(len(OUT_VECTOR) + 2):
            for behind in range(3):
                if 0 <= step - behind < len(OUT_VECTOR):
                    first, width = OUT_VECTOR[step - behind]
                    if behind < 2:
                        double(3 + behind, first // 16, (first + width) // 16)
                    else:
                        finish(first, width)
